import numpy as np
import ml_dtypes

BF16 = ml_dtypes.bfloat16


def bf(x):
    return np.asarray(x, np.float32).astype(BF16)


def f32(x):
    return np.asarray(x, np.float32)


def f64(x):
    return np.asarray(x).astype(np.float64)


def striped(idx):
    return np.tile(idx.reshape(-1, 16).T, (8, 1))


C, HC, S, N = 256, 128, 2048, 512


def gelu_tanh(v):
    return 0.5 * v * (1.0 + np.tanh(np.sqrt(2.0 / np.pi) * (v + 0.044715 * v**3)))


def arc_table():
    div = np.exp(np.arange(HC, dtype=np.float64) * (-np.log(10000.0) / HC))
    return div[:, None] * np.arange(N, dtype=np.float64)[None, :]


def setup_inputs():
    arc = arc_table()
    return {
        "emb": f32(0.1 * np.random.standard_normal((C, S))),
        "seq_dt": f32(np.random.uniform(0.0, 1.0, (1, N))),
        "wt": f32(np.random.uniform(-1.5, 1.5, (HC, 1))),
        "sin_arc": f32(np.sin(arc)),
        "cos_arc": f32(np.cos(arc)),
        "ws": bf(np.random.standard_normal((C, C)) / np.sqrt(C)),
        "bs": f32(0.1 * np.random.standard_normal((C, 1))),
        "offs": striped(np.random.permutation(np.tile(np.arange(S), 2))[:N]),
    }


def reference(emb, seq_dt, wt, sin_arc, cos_arc, ws, bs, offs):
    idx = offs[:16].T.reshape(-1)
    phi = f64(wt) * f64(seq_dt)
    sp, cp = np.sin(phi), np.cos(phi)
    sa, ca = f64(sin_arc), f64(cos_arc)
    pe = np.concatenate([sa * cp + ca * sp, ca * cp - sa * sp], axis=0)
    x = np.sqrt(C) * f64(emb)[:, idx] + pe
    return gelu_tanh(f64(ws).T @ x + f64(bs))

@@ -1,0 +1,119 @@
+import math
+
+import concourse.mybir as mybir
+
+F32 = mybir.dt.float32
+BF16 = mybir.dt.bfloat16
+U16 = mybir.dt.uint16
+FUNC = mybir.ActivationFunctionType
+ALU = mybir.AluOpType
+
+P = 128
+C = 256
+S = 2048
+N = 512
+BLOCKS = C // P
+SCALE = 16.0
+PIECES = 2
+W = N // PIECES
+
+FLOPS = 2 * C * C * N
+
+
+def tile_sahp_kernel(tc, emb, seq_dt, wt, sin_arc, cos_arc, ws, bs, offs, out):
+    nc = tc.nc
+    with (
+        tc.tile_pool(name="held", bufs=1) as held,
+        tc.psum_pool(name="psum", bufs=1) as psum,
+    ):
+        dt_row = held.tile([1, N], F32, name="dt_row")
+        nc.sync.dma_start(dt_row[:], seq_dt)
+        wt_row = held.tile([1, P], F32, name="wt_row")
+        nc.scalar.dma_start(wt_row[:], wt.rearrange("p o -> o p"))
+        sin_a = held.tile([P, N], F32, name="sin_a")
+        nc.sync.dma_start(sin_a[:], sin_arc)
+        cos_a = held.tile([P, N], F32, name="cos_a")
+        nc.scalar.dma_start(cos_a[:], cos_arc)
+        offsets = held.tile([P, N // 16], U16, name="offsets")
+        nc.sync.dma_start(offsets[:], offs)
+        table = []
+        for b in range(BLOCKS):
+            table_b = held.tile([P, S], F32, name=f"table{b}")
+            nc.sync.dma_start(table_b[:], emb[b * P : (b + 1) * P, :])
+            table.append(table_b)
+        weights = [held.tile([P, C], BF16, name=f"weights{kb}") for kb in range(BLOCKS)]
+        nc.scalar.dma_start(weights[0][:], ws[0:P, :])
+        nc.sync.dma_start(weights[1][:], ws[P : 2 * P, :])
+        bias = held.tile([P, BLOCKS], F32, name="bias")
+        with nc.allow_non_contiguous_dma(reason="256 biases, one to a partition"):
+            nc.sync.dma_start(bias[:], bs.rearrange("(mb p) o -> p (mb o)", p=P))
+
+        zero = held.tile([P, 1], F32, name="zero")
+        nc.vector.memset(zero[:], 0.0)
+        scratch = held.tile([P, 2], F32, name="scratch")
+        nc.scalar.activation(scratch[:, 0:1], zero[:], FUNC.Sin)
+
+        sum_a = held.tile([P, N], F32, name="sum_a")
+        nc.vector.tensor_tensor(sum_a[:], sin_a[:], cos_a[:], ALU.add)
+
+        def sine_of_phi_plus(name, phi, angle):
+            sine = held.tile([P, W], F32, name=name)
+            nc.scalar.activation(sine[:], phi[:], FUNC.Sin, bias=angle)
+            return sine
+
+        def product_16th(name, arc, factor, sine):
+            prod = held.tile([P, W], F32, name=name)
+            nc.vector.scalar_tensor_tensor(prod[:], arc, factor / SCALE, sine[:], ALU.mult, ALU.mult)
+            return prod
+
+        pe_16th = {}
+        for h in range(PIECES):
+            cols = slice(h * W, (h + 1) * W)
+            phi = psum.tile([P, W], F32, name=f"phi{h}")
+            nc.tensor.matmul(phi[:], wt_row[:], dt_row[:, cols], start=True, stop=True)
+            cos_p = sine_of_phi_plus(f"cos_p{h}", phi, math.pi / 2)
+            minus = sine_of_phi_plus(f"minus{h}", phi, -math.pi / 4)
+            plus = sine_of_phi_plus(f"plus{h}", phi, math.pi / 4)
+            k1 = product_16th(f"k1_{h}", sum_a[:, cols], 1.0, cos_p)
+            k2 = product_16th(f"k2_{h}", cos_a[:, cols], math.sqrt(2.0), minus)
+            k3 = product_16th(f"k3_{h}", sin_a[:, cols], math.sqrt(2.0), plus)
+            pe_16th[0, h] = held.tile([P, W], F32, name=f"pe0_{h}")
+            nc.vector.tensor_tensor(pe_16th[0, h][:], k1[:], k2[:], ALU.add)
+            pe_16th[1, h] = held.tile([P, W], F32, name=f"pe1_{h}")
+            nc.vector.tensor_tensor(pe_16th[1, h][:], k1[:], k3[:], ALU.subtract)
+        nc.scalar.activation(scratch[:, 1:2], plus[:, 0:1], FUNC.Gelu_apprx_tanh)
+
+        x = {}
+        for b in range(BLOCKS):
+            for h in range(PIECES):
+                picked = held.tile([P, W], F32, name=f"picked{b}_{h}")
+                nc.vector.tensor_tensor(
+                    picked[:],
+                    table[b][:].indirect(offsets[:, h * W // 16 : (h + 1) * W // 16]),
+                    pe_16th[b, h][:],
+                    ALU.add,
+                )
+                x[b, h] = held.tile([P, W], BF16, name=f"x{b}_{h}")
+                if (b, h) == (BLOCKS - 1, PIECES - 1):
+                    nc.vector.tensor_scalar(x[b, h][:], picked[:], SCALE, None, ALU.mult)
+                else:
+                    nc.scalar.activation(x[b, h][:], picked[:], FUNC.Copy, scale=SCALE)
+
+        acc = {}
+        for kb in range(BLOCKS):
+            for h in range(PIECES):
+                for mb in range(BLOCKS):
+                    if kb == 0:
+                        acc[mb, h] = psum.tile([P, W], F32, name=f"acc{mb}_{h}")
+                    nc.tensor.matmul(
+                        acc[mb, h][:],
+                        weights[kb][:, mb * P : (mb + 1) * P],
+                        x[kb, h][:],
+                        start=(kb == 0),
+                        stop=(kb == BLOCKS - 1),
+                    )
+        for h in range(PIECES):
+            for mb in range(BLOCKS):
+                y = held.tile([P, W], F32, name=f"y{mb}_{h}")
+                nc.scalar.activation(y[:], acc[mb, h][:], FUNC.Gelu_apprx_tanh, bias=bias[:, mb : mb + 1])
+                nc.sync.dma_start(out[mb * P : (mb + 1) * P, h * W : (h + 1) * W], y[:])

@@ -16,6 +16,7 @@ BLOCKS = C // P
 SCALE = 16.0
 PIECES = 2
 W = N // PIECES
+PE_STEPS = (slice(0, W // 2), slice(W // 2, W), slice(W, N))
 
 FLOPS = 2 * C * C * N
 
@@ -57,30 +58,33 @@ def tile_sahp_kernel(tc, emb, seq_dt, wt, sin_arc, cos_arc, ws, bs, offs, out):
         nc.vector.tensor_tensor(sum_a[:], sin_a[:], cos_a[:], ALU.add)
 
         def sine_of_phi_plus(name, phi, angle):
-            sine = held.tile([P, W], F32, name=name)
+            sine = held.tile(phi.shape, F32, name=name)
             nc.scalar.activation(sine[:], phi[:], FUNC.Sin, bias=angle)
             return sine
 
         def product_16th(name, arc, factor, sine):
-            prod = held.tile([P, W], F32, name=name)
+            prod = held.tile(sine.shape, F32, name=name)
             nc.vector.scalar_tensor_tensor(prod[:], arc, factor / SCALE, sine[:], ALU.mult, ALU.mult)
             return prod
 
         pe_16th = {}
-        for h in range(PIECES):
-            cols = slice(h * W, (h + 1) * W)
-            phi = psum.tile([P, W], F32, name=f"phi{h}")
+        for b in range(BLOCKS):
+            for h in range(PIECES):
+                pe_16th[b, h] = held.tile([P, W], F32, name=f"pe{b}_{h}")
+        for s, cols in enumerate(PE_STEPS):
+            n = cols.stop - cols.start
+            h = cols.start // W
+            part = slice(cols.start - h * W, cols.stop - h * W)
+            phi = psum.tile([P, n], F32, name=f"phi{s}")
             nc.tensor.matmul(phi[:], wt_row[:], dt_row[:, cols], start=True, stop=True)
-            cos_p = sine_of_phi_plus(f"cos_p{h}", phi, math.pi / 2)
-            minus = sine_of_phi_plus(f"minus{h}", phi, -math.pi / 4)
-            plus = sine_of_phi_plus(f"plus{h}", phi, math.pi / 4)
-            k1 = product_16th(f"k1_{h}", sum_a[:, cols], 1.0, cos_p)
-            k2 = product_16th(f"k2_{h}", cos_a[:, cols], math.sqrt(2.0), minus)
-            k3 = product_16th(f"k3_{h}", sin_a[:, cols], math.sqrt(2.0), plus)
-            pe_16th[0, h] = held.tile([P, W], F32, name=f"pe0_{h}")
-            nc.vector.tensor_tensor(pe_16th[0, h][:], k1[:], k2[:], ALU.add)
-            pe_16th[1, h] = held.tile([P, W], F32, name=f"pe1_{h}")
-            nc.vector.tensor_tensor(pe_16th[1, h][:], k1[:], k3[:], ALU.subtract)
+            cos_p = sine_of_phi_plus(f"cos_p{s}", phi, math.pi / 2)
+            minus = sine_of_phi_plus(f"minus{s}", phi, -math.pi / 4)
+            plus = sine_of_phi_plus(f"plus{s}", phi, math.pi / 4)
+            k1 = product_16th(f"k1_{s}", sum_a[:, cols], 1.0, cos_p)
+            k2 = product_16th(f"k2_{s}", cos_a[:, cols], math.sqrt(2.0), minus)
+            k3 = product_16th(f"k3_{s}", sin_a[:, cols], math.sqrt(2.0), plus)
+            nc.vector.tensor_tensor(pe_16th[0, h][:, part], k1[:], k2[:], ALU.add)
+            nc.vector.tensor_tensor(pe_16th[1, h][:, part], k1[:], k3[:], ALU.subtract)
         nc.scalar.activation(scratch[:, 1:2], plus[:, 0:1], FUNC.Gelu_apprx_tanh)
 
         x = {}

@@ -42,9 +42,11 @@ def tile_sahp_kernel(tc, emb, seq_dt, wt, sin_arc, cos_arc, ws, bs, offs, out):
             table_b = held.tile([P, S], F32, name=f"table{b}")
             nc.sync.dma_start(table_b[:], emb[b * P : (b + 1) * P, :])
             table.append(table_b)
-        weights = [held.tile([P, C], BF16, name=f"weights{kb}") for kb in range(BLOCKS)]
-        nc.scalar.dma_start(weights[0][:], ws[0:P, :])
-        nc.sync.dma_start(weights[1][:], ws[P : 2 * P, :])
+        weights = []
+        for kb in range(BLOCKS):
+            weights_kb = held.tile([P, C], BF16, name=f"weights{kb}")
+            nc.sync.dma_start(weights_kb[:], ws[kb * P : (kb + 1) * P, :])
+            weights.append(weights_kb)
         bias = held.tile([P, BLOCKS], F32, name="bias")
         with nc.allow_non_contiguous_dma(reason="256 biases, one to a partition"):
             nc.sync.dma_start(bias[:], bs.rearrange("(mb p) o -> p (mb o)", p=P))

@@ -16,7 +16,7 @@ BLOCKS = C // P
 SCALE = 16.0
 PIECES = 2
 W = N // PIECES
-PE_STEPS = (slice(0, W // 2), slice(W // 2, W), slice(W, N))
+PE_STEPS = [slice(n, n + W // 2) for n in range(0, N, W // 2)]
 
 FLOPS = 2 * C * C * N
 
@@ -32,9 +32,11 @@ def tile_sahp_kernel(tc, emb, seq_dt, wt, sin_arc, cos_arc, ws, bs, offs, out):
         wt_row = held.tile([1, P], F32, name="wt_row")
         nc.scalar.dma_start(wt_row[:], wt.rearrange("p o -> o p"))
         sin_a = held.tile([P, N], F32, name="sin_a")
-        nc.sync.dma_start(sin_a[:], sin_arc)
         cos_a = held.tile([P, N], F32, name="cos_a")
-        nc.scalar.dma_start(cos_a[:], cos_arc)
+        for h in range(PIECES):
+            cols = slice(h * W, (h + 1) * W)
+            nc.sync.dma_start(sin_a[:, cols], sin_arc[:, cols])
+            nc.scalar.dma_start(cos_a[:, cols], cos_arc[:, cols])
         offsets = held.tile([P, N // 16], U16, name="offsets")
         nc.sync.dma_start(offsets[:], offs)
         table = []
@@ -57,7 +59,9 @@ def tile_sahp_kernel(tc, emb, seq_dt, wt, sin_arc, cos_arc, ws, bs, offs, out):
         nc.scalar.activation(scratch[:, 0:1], zero[:], FUNC.Sin)
 
         sum_a = held.tile([P, N], F32, name="sum_a")
-        nc.vector.tensor_tensor(sum_a[:], sin_a[:], cos_a[:], ALU.add)
+        for h in range(PIECES):
+            cols = slice(h * W, (h + 1) * W)
+            nc.vector.tensor_tensor(sum_a[:, cols], sin_a[:, cols], cos_a[:, cols], ALU.add)
 
         def sine_of_phi_plus(name, phi, angle):
             sine = held.tile(phi.shape, F32, name=name)

@@ -14,9 +14,17 @@ S = 2048
 N = 512
 BLOCKS = C // P
 SCALE = 16.0
-PIECES = 2
-W = N // PIECES
-PE_STEPS = [slice(n, n + W // 2) for n in range(0, N, W // 2)]
+
+
+def cut(*widths):
+    ends = [sum(widths[: n + 1]) for n in range(len(widths))]
+    return [slice(end - width, end) for end, width in zip(ends, widths)]
+
+
+HALVES = cut(N // 2, N // 2)
+PE_RANGES = cut(N // 4, N // 4, N // 4, N // 4)
+X_RANGES = [HALVES, cut(N // 4, N // 4, N // 2)]
+
 
 FLOPS = 2 * C * C * N
 
@@ -33,8 +41,7 @@ def tile_sahp_kernel(tc, emb, seq_dt, wt, sin_arc, cos_arc, ws, bs, offs, out):
         nc.scalar.dma_start(wt_row[:], wt.rearrange("p o -> o p"))
         sin_a = held.tile([P, N], F32, name="sin_a")
         cos_a = held.tile([P, N], F32, name="cos_a")
-        for h in range(PIECES):
-            cols = slice(h * W, (h + 1) * W)
+        for cols in HALVES:
             nc.sync.dma_start(sin_a[:, cols], sin_arc[:, cols])
             nc.scalar.dma_start(cos_a[:, cols], cos_arc[:, cols])
         offsets = held.tile([P, N // 16], U16, name="offsets")
@@ -59,8 +66,7 @@ def tile_sahp_kernel(tc, emb, seq_dt, wt, sin_arc, cos_arc, ws, bs, offs, out):
         nc.scalar.activation(scratch[:, 0:1], zero[:], FUNC.Sin)
 
         sum_a = held.tile([P, N], F32, name="sum_a")
-        for h in range(PIECES):
-            cols = slice(h * W, (h + 1) * W)
+        for cols in HALVES:
             nc.vector.tensor_tensor(sum_a[:, cols], sin_a[:, cols], cos_a[:, cols], ALU.add)
 
         def sine_of_phi_plus(name, phi, angle):
@@ -73,15 +79,15 @@ def tile_sahp_kernel(tc, emb, seq_dt, wt, sin_arc, cos_arc, ws, bs, offs, out):
             nc.vector.scalar_tensor_tensor(prod[:], arc, factor / SCALE, sine[:], ALU.mult, ALU.mult)
             return prod
 
-        pe_16th = {}
-        for b in range(BLOCKS):
-            for h in range(PIECES):
-                pe_16th[b, h] = held.tile([P, W], F32, name=f"pe{b}_{h}")
-        for s, cols in enumerate(PE_STEPS):
-            n = cols.stop - cols.start
-            h = cols.start // W
-            part = slice(cols.start - h * W, cols.stop - h * W)
-            phi = psum.tile([P, n], F32, name=f"phi{s}")
+        banks_used = []
+
+        def next_bank():
+            banks_used.append(len(banks_used) % 8)
+            return f"bank{banks_used[-1]}"
+
+        pe_16th = [held.tile([P, N], F32, name=f"pe{b}") for b in range(BLOCKS)]
+        for s, cols in enumerate(PE_RANGES):
+            phi = psum.tile([P, cols.stop - cols.start], F32, name=f"phi{s}", tag=next_bank())
             nc.tensor.matmul(phi[:], wt_row[:], dt_row[:, cols], start=True, stop=True)
             cos_p = sine_of_phi_plus(f"cos_p{s}", phi, math.pi / 2)
             minus = sine_of_phi_plus(f"minus{s}", phi, -math.pi / 4)
@@ -89,41 +95,44 @@ def tile_sahp_kernel(tc, emb, seq_dt, wt, sin_arc, cos_arc, ws, bs, offs, out):
             k1 = product_16th(f"k1_{s}", sum_a[:, cols], 1.0, cos_p)
             k2 = product_16th(f"k2_{s}", cos_a[:, cols], math.sqrt(2.0), minus)
             k3 = product_16th(f"k3_{s}", sin_a[:, cols], math.sqrt(2.0), plus)
-            nc.vector.tensor_tensor(pe_16th[0, h][:, part], k1[:], k2[:], ALU.add)
-            nc.vector.tensor_tensor(pe_16th[1, h][:, part], k1[:], k3[:], ALU.subtract)
+            nc.vector.tensor_tensor(pe_16th[0][:, cols], k1[:], k2[:], ALU.add)
+            nc.vector.tensor_tensor(pe_16th[1][:, cols], k1[:], k3[:], ALU.subtract)
         nc.scalar.activation(scratch[:, 1:2], plus[:, 0:1], FUNC.Gelu_apprx_tanh)
 
-        x = {}
+        x = []
         for b in range(BLOCKS):
-            for h in range(PIECES):
-                picked = held.tile([P, W], F32, name=f"picked{b}_{h}")
+            picked = held.tile([P, N], F32, name=f"picked{b}")
+            x_b = held.tile([P, N], BF16, name=f"x{b}")
+            for cols in X_RANGES[b]:
                 nc.vector.tensor_tensor(
-                    picked[:],
-                    table[b][:].indirect(offsets[:, h * W // 16 : (h + 1) * W // 16]),
-                    pe_16th[b, h][:],
+                    picked[:, cols],
+                    table[b][:].indirect(offsets[:, cols.start // 16 : cols.stop // 16]),
+                    pe_16th[b][:, cols],
                     ALU.add,
                 )
-                x[b, h] = held.tile([P, W], BF16, name=f"x{b}_{h}")
-                if (b, h) == (BLOCKS - 1, PIECES - 1):
-                    nc.vector.tensor_scalar(x[b, h][:], picked[:], SCALE, None, ALU.mult)
+                if b == BLOCKS - 1 and cols.stop == N:
+                    nc.vector.tensor_scalar(x_b[:, cols], picked[:, cols], SCALE, None, ALU.mult)
                 else:
-                    nc.scalar.activation(x[b, h][:], picked[:], FUNC.Copy, scale=SCALE)
+                    nc.scalar.activation(x_b[:, cols], picked[:, cols], FUNC.Copy, scale=SCALE)
+            x.append(x_b)
 
         acc = {}
         for kb in range(BLOCKS):
-            for h in range(PIECES):
+            for r, cols in enumerate(X_RANGES[-1]):
                 for mb in range(BLOCKS):
                     if kb == 0:
-                        acc[mb, h] = psum.tile([P, W], F32, name=f"acc{mb}_{h}")
+                        acc[mb, r] = psum.tile([P, cols.stop - cols.start], F32, name=f"acc{mb}_{r}", tag=next_bank())
                     nc.tensor.matmul(
-                        acc[mb, h][:],
+                        acc[mb, r][:],
                         weights[kb][:, mb * P : (mb + 1) * P],
-                        x[kb, h][:],
+                        x[kb][:, cols],
                         start=(kb == 0),
                         stop=(kb == BLOCKS - 1),
                     )
-        for h in range(PIECES):
+        y = [held.tile([P, N], F32, name=f"y{mb}") for mb in range(BLOCKS)]
+        for r, cols in enumerate(X_RANGES[-1]):
             for mb in range(BLOCKS):
-                y = held.tile([P, W], F32, name=f"y{mb}_{h}")
-                nc.scalar.activation(y[:], acc[mb, h][:], FUNC.Gelu_apprx_tanh, bias=bias[:, mb : mb + 1])
-                nc.sync.dma_start(out[mb * P : (mb + 1) * P, h * W : (h + 1) * W], y[:])
+                nc.scalar.activation(y[mb][:, cols], acc[mb, r][:], FUNC.Gelu_apprx_tanh, bias=bias[:, mb : mb + 1])
+                for half in HALVES:
+                    if half.stop == cols.stop:
+                        nc.sync.dma_start(out[mb * P : (mb + 1) * P, half], y[mb][:, half])

@@ -22,7 +22,7 @@ def cut(*widths):
 
 
 HALVES = cut(N // 2, N // 2)
-PE_RANGES = cut(N // 4, N // 4, N // 4, N // 4)
+PE_RANGES = cut(N // 4, N // 4, N // 2)
 X_RANGES = [HALVES, cut(N // 4, N // 4, N // 2)]
 
 

import math

import concourse.mybir as mybir

F32 = mybir.dt.float32
BF16 = mybir.dt.bfloat16
U16 = mybir.dt.uint16
FUNC = mybir.ActivationFunctionType
ALU = mybir.AluOpType

P = 128
C = 256
S = 2048
N = 512
BLOCKS = C // P
SCALE = 16.0


def cut(*widths):
    ends = [sum(widths[: n + 1]) for n in range(len(widths))]
    return [slice(end - width, end) for end, width in zip(ends, widths)]


HALVES = cut(N // 2, N // 2)
PE_RANGES = cut(N // 4, N // 4, N // 2)
X_RANGES = [HALVES, cut(N // 4, N // 4, N // 2)]


FLOPS = 2 * C * C * N


def tile_sahp_kernel(tc, emb, seq_dt, wt, sin_arc, cos_arc, ws, bs, offs, out):
    nc = tc.nc
    with (
        tc.tile_pool(name="held", bufs=1) as held,
        tc.psum_pool(name="psum", bufs=1) as psum,
    ):
        dt_row = held.tile([1, N], F32, name="dt_row")
        nc.sync.dma_start(dt_row[:], seq_dt)
        wt_row = held.tile([1, P], F32, name="wt_row")
        nc.scalar.dma_start(wt_row[:], wt.rearrange("p o -> o p"))
        sin_a = held.tile([P, N], F32, name="sin_a")
        cos_a = held.tile([P, N], F32, name="cos_a")
        for cols in HALVES:
            nc.sync.dma_start(sin_a[:, cols], sin_arc[:, cols])
            nc.scalar.dma_start(cos_a[:, cols], cos_arc[:, cols])
        offsets = held.tile([P, N // 16], U16, name="offsets")
        nc.sync.dma_start(offsets[:], offs)
        table = []
        for b in range(BLOCKS):
            table_b = held.tile([P, S], F32, name=f"table{b}")
            nc.sync.dma_start(table_b[:], emb[b * P : (b + 1) * P, :])
            table.append(table_b)
        weights = []
        for kb in range(BLOCKS):
            weights_kb = held.tile([P, C], BF16, name=f"weights{kb}")
            nc.sync.dma_start(weights_kb[:], ws[kb * P : (kb + 1) * P, :])
            weights.append(weights_kb)
        bias = held.tile([P, BLOCKS], F32, name="bias")
        with nc.allow_non_contiguous_dma(reason="256 biases, one to a partition"):
            nc.sync.dma_start(bias[:], bs.rearrange("(mb p) o -> p (mb o)", p=P))

        zero = held.tile([P, 1], F32, name="zero")
        nc.vector.memset(zero[:], 0.0)
        scratch = held.tile([P, 2], F32, name="scratch")
        nc.scalar.activation(scratch[:, 0:1], zero[:], FUNC.Sin)

        sum_a = held.tile([P, N], F32, name="sum_a")
        for cols in HALVES:
            nc.vector.tensor_tensor(sum_a[:, cols], sin_a[:, cols], cos_a[:, cols], ALU.add)

        def sine_of_phi_plus(name, phi, angle):
            sine = held.tile(phi.shape, F32, name=name)
            nc.scalar.activation(sine[:], phi[:], FUNC.Sin, bias=angle)
            return sine

        def product_16th(name, arc, factor, sine):
            prod = held.tile(sine.shape, F32, name=name)
            nc.vector.scalar_tensor_tensor(prod[:], arc, factor / SCALE, sine[:], ALU.mult, ALU.mult)
            return prod

        banks_used = []

        def next_bank():
            banks_used.append(len(banks_used) % 8)
            return f"bank{banks_used[-1]}"

        pe_16th = [held.tile([P, N], F32, name=f"pe{b}") for b in range(BLOCKS)]
        for s, cols in enumerate(PE_RANGES):
            phi = psum.tile([P, cols.stop - cols.start], F32, name=f"phi{s}", tag=next_bank())
            nc.tensor.matmul(phi[:], wt_row[:], dt_row[:, cols], start=True, stop=True)
            cos_p = sine_of_phi_plus(f"cos_p{s}", phi, math.pi / 2)
            minus = sine_of_phi_plus(f"minus{s}", phi, -math.pi / 4)
            plus = sine_of_phi_plus(f"plus{s}", phi, math.pi / 4)
            k1 = product_16th(f"k1_{s}", sum_a[:, cols], 1.0, cos_p)
            k2 = product_16th(f"k2_{s}", cos_a[:, cols], math.sqrt(2.0), minus)
            k3 = product_16th(f"k3_{s}", sin_a[:, cols], math.sqrt(2.0), plus)
            nc.vector.tensor_tensor(pe_16th[0][:, cols], k1[:], k2[:], ALU.add)
            nc.vector.tensor_tensor(pe_16th[1][:, cols], k1[:], k3[:], ALU.subtract)
        nc.scalar.activation(scratch[:, 1:2], plus[:, 0:1], FUNC.Gelu_apprx_tanh)

        x = []
        for b in range(BLOCKS):
            picked = held.tile([P, N], F32, name=f"picked{b}")
            x_b = held.tile([P, N], BF16, name=f"x{b}")
            for cols in X_RANGES[b]:
                nc.vector.tensor_tensor(
                    picked[:, cols],
                    table[b][:].indirect(offsets[:, cols.start // 16 : cols.stop // 16]),
                    pe_16th[b][:, cols],
                    ALU.add,
                )
                if b == BLOCKS - 1 and cols.stop == N:
                    nc.vector.tensor_scalar(x_b[:, cols], picked[:, cols], SCALE, None, ALU.mult)
                else:
                    nc.scalar.activation(x_b[:, cols], picked[:, cols], FUNC.Copy, scale=SCALE)
            x.append(x_b)

        acc = {}
        for kb in range(BLOCKS):
            for r, cols in enumerate(X_RANGES[-1]):
                for mb in range(BLOCKS):
                    if kb == 0:
                        acc[mb, r] = psum.tile([P, cols.stop - cols.start], F32, name=f"acc{mb}_{r}", tag=next_bank())
                    nc.tensor.matmul(
                        acc[mb, r][:],
                        weights[kb][:, mb * P : (mb + 1) * P],
                        x[kb][:, cols],
                        start=(kb == 0),
                        stop=(kb == BLOCKS - 1),
                    )
        y = [held.tile([P, N], F32, name=f"y{mb}") for mb in range(BLOCKS)]
        for r, cols in enumerate(X_RANGES[-1]):
            for mb in range(BLOCKS):
                nc.scalar.activation(y[mb][:, cols], acc[mb, r][:], FUNC.Gelu_apprx_tanh, bias=bias[:, mb : mb + 1])
                for half in HALVES:
                    if half.stop == cols.stop:
                        nc.sync.dma_start(out[mb * P : (mb + 1) * P, half], y[mb][:, half])
